import numpy as np
import ml_dtypes


def mxq(x, axis, fmt="e4m3"):
    dtype, down = {"e4m3": (ml_dtypes.float8_e4m3fn, 7), "e5m2": (ml_dtypes.float8_e5m2, 14)}[fmt]
    v = np.moveaxis(np.asarray(x, np.float32).astype(ml_dtypes.bfloat16).astype(np.float64), axis, -1)
    blocks = v.reshape(v.shape[:-1] + (-1, 32))
    amax = np.abs(blocks).max(-1, keepdims=True)
    byte = np.maximum(np.where(amax > 0, np.frexp(amax)[1] - 1 + 127, 0) - down, 1)
    scale = np.exp2(byte - 127.0)
    codes = (blocks / scale).astype(np.float32).astype(dtype).astype(np.float64)
    return np.moveaxis((codes * scale).reshape(v.shape), -1, axis)


WIDE = False


def mx_kscale(k):
    if not WIDE:
        return np.ones(k)
    levels = np.array([10, -10, 5, -5, 0])
    a = np.random.permutation(np.resize(levels, k // 512 * 4)).reshape(k // 512, 4)
    idx = np.arange(k)
    return np.exp2(a[idx // 512, idx % 128 // 32])


BF16 = ml_dtypes.bfloat16


def bf(x):
    return np.asarray(x, np.float32).astype(BF16)


def f64(x):
    return np.asarray(x).astype(np.float64)


B, K, H, D = 2048, 512, 512, 2
C = 0.2
HALF_LOG_2PI = 0.5 * np.log(2.0 * np.pi)


def log_softmax(v, axis):
    v = v - v.max(axis=axis, keepdims=True)
    return v - np.log(np.exp(v).sum(axis=axis, keepdims=True))


def logsumexp(v, axis):
    m = v.max(axis=axis, keepdims=True)
    return np.log(np.exp(v - m).sum(axis=axis)) + np.squeeze(m, axis)


def contract(xq, vq):
    return (xq.transpose(2, 0, 1) @ vq.transpose(2, 1, 0)).transpose(1, 2, 0)


def setup_inputs():
    s = mx_kscale(H)[None, :, None]
    r = 1.0 / np.sqrt(H)
    return {
        "x": bf(np.random.standard_normal((B, H, D)) * s),
        "input_var": bf(np.random.standard_normal((B, D)) * C),
        "V_alpha": bf(np.random.standard_normal((K, H, D)) * r / s),
        "V_mu": bf(np.random.standard_normal((K, H, D)) * C * r / s),
        "V_sigma": bf(np.random.standard_normal((K, H, D)) * 0.5 * r / s),
        "b_alpha": bf(np.random.standard_normal((K, D)) * 0.7),
        "b_mu": bf(np.random.standard_normal((K, D)) * 0.5 * C),
        "b_sigma": bf(np.log(C) + np.random.standard_normal((K, D)) * 0.3),
    }


def reference(x, input_var, V_alpha, V_mu, V_sigma, b_alpha, b_mu, b_sigma):
    xq = mxq(f64(x), 1, "e4m3")
    exp_alpha = contract(xq, mxq(f64(V_alpha), 1, "e4m3")) + f64(b_alpha)
    log_alpha = log_softmax(exp_alpha, 1)
    mu = contract(xq, mxq(f64(V_mu), 1, "e4m3")) + f64(b_mu)
    log_sigma = np.clip(contract(xq, mxq(f64(V_sigma), 1, "e4m3")) + f64(b_sigma), -20.0, 20.0)
    sigma = np.exp(log_sigma)
    y = f64(input_var)[:, None, :]
    log_p = -0.5 * np.square((y - mu) / sigma) + log_alpha - HALF_LOG_2PI - log_sigma
    return np.sum(logsumexp(log_p, 1), axis=1)

@@ -1,0 +1,337 @@
+import math
+from contextlib import ExitStack
+
+import concourse.mybir as mybir
+from concourse.masks import make_identity
+
+F32 = mybir.dt.float32
+BF16 = mybir.dt.bfloat16
+U32 = mybir.dt.uint32
+U8 = mybir.dt.uint8
+FP8X4 = mybir.dt.float8_e4m3fn_x4
+ALU = mybir.AluOpType
+ACT = mybir.ActivationFunctionType
+AXIS = mybir.AxisListType
+
+P = 128
+PACK = 4
+B, K, H, D = 2048, 512, 512, 2
+H_LOW = H // PACK
+ROWS = P // PACK
+N_COLS = 512
+BANK_BF16 = 1024
+KT = K // P
+N_CHUNKS = B // N_COLS
+BLOCKS = N_COLS // P
+STEPS = N_CHUNKS * D * KT
+X_BANKS = 2 * D
+LAG = KT + 1
+CLIP = 20.0
+SIGMA, MU, ALPHA = 0, 1, 2
+
+FLOPS = 2 * B * K * H * D * 3
+
+
+def tile_rnadeoutputlayer_t_kernel(
+    tc, x, input_var, V_alpha, V_mu, V_sigma, b_alpha, b_mu, b_sigma, out
+):
+    nc = tc.nc
+    weights = (V_sigma, V_mu, V_alpha)
+    biases = (b_sigma, b_mu, b_alpha)
+
+    with ExitStack() as ctx:
+        const = ctx.enter_context(tc.tile_pool(name="const", bufs=1))
+        raw = ctx.enter_context(tc.tile_pool(name="raw", bufs=1))
+        stage = ctx.enter_context(tc.tile_pool(name="stage", bufs=3))
+        work = ctx.enter_context(tc.tile_pool(name="work", bufs=3))
+        keep = ctx.enter_context(tc.tile_pool(name="keep", bufs=3 * KT))
+        mx_psum = ctx.enter_context(tc.psum_pool(name="mx_psum", bufs=1))
+        tp_psum = ctx.enter_context(tc.psum_pool(name="tp_psum", bufs=5))
+
+        x_rows = x.rearrange("b (t hl) d -> (b t) (hl d)", t=PACK).rearrange(
+            "(r p) c -> p r c", p=P
+        )
+        x_tiles_per_chunk = N_COLS // ROWS
+        v_tiles_per_kt = P // ROWS
+
+        def load_x(chunk):
+            x_raw = raw.tile([P, x_tiles_per_chunk, H_LOW, D], BF16, name="x_raw%d" % chunk)
+            half = x_tiles_per_chunk // 2
+            for part in range(2):
+                first = chunk * x_tiles_per_chunk + part * half
+                nc.sync.dma_start(
+                    out=x_raw[:, part * half : (part + 1) * half].rearrange("p r hl d -> p r (hl d)"),
+                    in_=x_rows[:, first : first + half, :],
+                )
+            return x_raw
+
+        def load_weight(w, kt):
+            v_rows = weights[w].rearrange("k (t hl) d -> (k t) (hl d)", t=PACK).rearrange(
+                "(r p) c -> p r c", p=P
+            )
+            v_raw = raw.tile([P, v_tiles_per_kt, H_LOW, D], BF16, name="v_raw%d_%d" % (w, kt))
+            nc.sync.dma_start(
+                out=v_raw[:].rearrange("p r hl d -> p r (hl d)"),
+                in_=v_rows[:, kt * v_tiles_per_kt : (kt + 1) * v_tiles_per_kt, :],
+            )
+            return v_raw
+
+        v_raws = {}
+        x_raws = {}
+        v_raws[(SIGMA, 0)] = load_weight(SIGMA, 0)
+        x_raws[0] = load_x(0)
+        v_raws[(MU, 0)] = load_weight(MU, 0)
+        v_raws[(ALPHA, 0)] = load_weight(ALPHA, 0)
+        for kt in range(1, KT):
+            for w in (SIGMA, MU, ALPHA):
+                v_raws[(w, kt)] = load_weight(w, kt)
+        for chunk in range(1, N_CHUNKS):
+            x_raws[chunk] = load_x(chunk)
+
+        bias_rows = const.tile([P, P, D], BF16)
+        nc.vector.memset(bias_rows[:], 0.0)
+        for w in (SIGMA, MU, ALPHA):
+            nc.scalar.dma_start(
+                out=bias_rows[KT * w : KT * (w + 1)].rearrange("kt kl d -> kt (kl d)"),
+                in_=biases[w].rearrange("(kt kl) d -> kt (kl d)", kt=KT),
+            )
+        y_tiles = []
+        for chunk in range(N_CHUNKS):
+            y_all = const.tile([P, N_COLS, D], BF16, name="y_all%d" % chunk)
+            nc.scalar.dma_start(
+                out=y_all[:].rearrange("p b d -> p (b d)"),
+                in_=input_var[chunk * N_COLS : (chunk + 1) * N_COLS, :]
+                .rearrange("b d -> (b d)")
+                .partition_broadcast(P),
+            )
+            y_tiles.append(y_all)
+
+        ident_bf16 = const.tile([P, P], BF16)
+        make_identity(nc, ident_bf16[:])
+        ident_f32 = const.tile([P, P], F32)
+        make_identity(nc, ident_f32[:])
+
+        warm = const.tile([P, 2], F32)
+        nc.vector.memset(warm[:], 0.0)
+        nc.scalar.activation(out=warm[:, 1:2], in_=warm[:, 0:1], func=ACT.Exp)
+
+        result = const.tile([P, P], F32)
+        nc.vector.memset(result[:], 0.0)
+
+        bias_bank = tp_psum.tile([P, D, P], BF16, tag="bank")
+        for d in range(D):
+            nc.tensor.transpose(out=bias_bank[:, d, :], in_=bias_rows[:, :, d], identity=ident_bf16[:])
+        bias = const.tile([P, D, 3 * KT], F32)
+        nc.vector.tensor_copy(out=bias[:], in_=bias_bank[:, :, 0 : 3 * KT])
+        b_sig = bias[:, :, KT * SIGMA : KT * (SIGMA + 1)]
+        neg_b_sig = const.tile([P, D, KT], F32)
+        nc.vector.tensor_scalar(out=neg_b_sig[:], in0=b_sig, scalar1=-1.0, scalar2=None, op0=ALU.mult)
+        clip_low = const.tile([P, D, KT], F32)
+        nc.vector.tensor_scalar(
+            out=clip_low[:], in0=b_sig, scalar1=-1.0, scalar2=-CLIP, op0=ALU.mult, op1=ALU.add
+        )
+        clip_high = const.tile([P, D, KT], F32)
+        nc.vector.tensor_scalar(
+            out=clip_high[:], in0=b_sig, scalar1=-1.0, scalar2=CLIP, op0=ALU.mult, op1=ALU.add
+        )
+
+        n_blocks = B // P
+        neg_max = const.tile([P, 2, D, n_blocks], F32)
+        exp_sum = const.tile([P, 2, D, n_blocks], F32)
+
+        v_codes = [
+            const.tile([P, KT, D, P], U32, name="v_codes%d" % w, align_bytes=64) for w in range(3)
+        ]
+        v_scales = [
+            const.tile([P, KT, D, P], U8, name="v_scales%d" % w, align_bytes=64) for w in range(3)
+        ]
+
+        def empty_bank(n, grouped_part, bank):
+            if n % 2 == 0:
+                nc.vector.tensor_copy(out=grouped_part, in_=bank)
+            else:
+                nc.scalar.copy(out=grouped_part, in_=bank)
+
+        def quantise_weight(w, kt):
+            v_raw = v_raws[(w, kt)]
+            bank = tp_psum.tile([P, D, v_tiles_per_kt, P], BF16, tag="bank")
+            for d in range(D):
+                for r in range(v_tiles_per_kt):
+                    nc.tensor.transpose(
+                        out=bank[:, d, r, :], in_=v_raw[:, r, :, d], identity=ident_bf16[:]
+                    )
+            v_grouped = stage.tile([P, BANK_BF16], BF16, align_bytes=64)
+            empty_bank(w, v_grouped[:], bank[:].rearrange("p d r c -> p (d r c)"))
+            nc.vector.quantize_mx(
+                out=v_codes[w][:, kt].rearrange("p d k -> p (d k)").bitcast(FP8X4),
+                scales=v_scales[w][:, kt].rearrange("p d k -> p (d k)"),
+                in_=v_grouped[:],
+            )
+
+        x_grouped = {}
+        x_codes = {}
+        x_scales = {}
+
+        def quantise_x_bank(n):
+            chunk, d, half = n // X_BANKS, (n % X_BANKS) // 2, n % 2
+            group = (chunk, d)
+            tiles = x_tiles_per_chunk // 2
+            bank = tp_psum.tile([P, tiles, P], BF16, tag="bank")
+            for r in range(tiles):
+                nc.tensor.transpose(
+                    out=bank[:, r, :], in_=x_raws[chunk][:, half * tiles + r, :, d], identity=ident_bf16[:]
+                )
+            if half == 0:
+                x_grouped[group] = stage.tile(
+                    [P, 2, BANK_BF16], BF16, name="x_grouped", align_bytes=64
+                )
+            empty_bank(n, x_grouped[group][:, half, :], bank[:].rearrange("p r c -> p (r c)"))
+            if half == 1:
+                x_codes[group] = stage.tile([P, N_COLS], U32, name="x_codes", align_bytes=64)
+                x_scales[group] = stage.tile([P, N_COLS], U8, name="x_scales", align_bytes=64)
+                nc.vector.quantize_mx(
+                    out=x_codes[group][:].bitcast(FP8X4),
+                    scales=x_scales[group][:],
+                    in_=x_grouped[group][:].rearrange("p h c -> p (h c)"),
+                )
+
+        t_tiles = {}
+        a_tiles = {}
+
+        def product(w, kt, group, tag):
+            acc = mx_psum.tile([P, N_COLS], F32, name="acc_" + tag, tag=tag)
+            nc.tensor.matmul_mx(
+                out=acc[:],
+                lhsT=v_codes[w][:, kt, group[1], :].bitcast(FP8X4),
+                lhsT_scale=v_scales[w][:, kt, group[1], :],
+                rhs=x_codes[group][:].bitcast(FP8X4),
+                rhs_scale=x_scales[group][:],
+                start=True,
+                stop=True,
+            )
+            return acc
+
+        def density_tile(step):
+            chunk, d, kt = step // (D * KT), (step // KT) % D, step % KT
+            group = (chunk, d)
+            column = slice(kt, kt + 1)
+
+            sigma_acc = product(SIGMA, kt, group, "sigma")
+            clipped = work.tile([P, N_COLS], F32)
+            nc.vector.tensor_scalar(
+                out=clipped[:],
+                in0=sigma_acc[:],
+                scalar1=clip_low[:, d, column],
+                scalar2=clip_high[:, d, column],
+                op0=ALU.max,
+                op1=ALU.min,
+            )
+            inv_sigma = work.tile([P, N_COLS], F32)
+            nc.scalar.activation(
+                out=inv_sigma[:], in_=clipped[:], func=ACT.Exp, bias=neg_b_sig[:, d, column], scale=-1.0
+            )
+
+            mu_acc = product(MU, kt, group, "mu")
+            distance = work.tile([P, N_COLS], F32)
+            nc.vector.scalar_tensor_tensor(
+                out=distance[:],
+                in0=mu_acc[:],
+                scalar=bias[:, d, KT * MU + kt : KT * MU + kt + 1],
+                in1=y_tiles[chunk][:, :, d],
+                op0=ALU.add,
+                op1=ALU.subtract,
+            )
+            z = work.tile([P, N_COLS], F32)
+            nc.gpsimd.tensor_tensor(out=z[:], in0=distance[:], in1=inv_sigma[:], op=ALU.mult)
+            half_z2 = work.tile([P, N_COLS], F32)
+            nc.scalar.activation(out=half_z2[:], in_=z[:], func=ACT.Square, scale=math.sqrt(0.5))
+            penalty = work.tile([P, N_COLS], F32)
+            nc.gpsimd.tensor_tensor(out=penalty[:], in0=clipped[:], in1=half_z2[:], op=ALU.add)
+
+            alpha_acc = product(ALPHA, kt, group, "alpha")
+            a_tile = keep.tile([P, N_COLS], F32)
+            nc.scalar.activation(
+                out=a_tile[:],
+                in_=alpha_acc[:],
+                func=ACT.Identity,
+                bias=bias[:, d, KT * ALPHA + kt : KT * ALPHA + kt + 1],
+                scale=1.0,
+            )
+            t_tile = keep.tile([P, N_COLS], F32)
+            nc.vector.scalar_tensor_tensor(
+                out=t_tile[:],
+                in0=a_tile[:],
+                scalar=neg_b_sig[:, d, column],
+                in1=penalty[:],
+                op0=ALU.add,
+                op1=ALU.subtract,
+            )
+            t_tiles[step] = t_tile
+            a_tiles[step] = a_tile
+
+        def reduce_block(block):
+            first_step = (block // BLOCKS) * KT
+            chunk, d, j = block // (D * BLOCKS), (block // BLOCKS) % D, block % BLOCKS
+            column = chunk * BLOCKS + j
+            samples = slice(j * P, (j + 1) * P)
+            for kind, tiles in enumerate((t_tiles, a_tiles)):
+                turned = tp_psum.tile([P, K], F32, tag="bank")
+                for kt in range(KT):
+                    nc.tensor.transpose(
+                        out=turned[:, kt * P : (kt + 1) * P],
+                        in_=tiles[first_step + kt][:, samples],
+                        identity=ident_f32[:],
+                    )
+                nc.vector.tensor_reduce(
+                    out=neg_max[:, kind, d, column : column + 1],
+                    in_=turned[:],
+                    axis=AXIS.X,
+                    op=ALU.max,
+                    negate=True,
+                )
+                unread = work.tile([P, K], F32)
+                nc.scalar.activation(
+                    out=unread[:],
+                    in_=turned[:],
+                    func=ACT.Exp,
+                    bias=neg_max[:, kind, d, column : column + 1],
+                    scale=1.0,
+                    accum_out=exp_sum[:, kind, d, column : column + 1],
+                )
+
+        quantise_weight(SIGMA, 0)
+        quantise_x_bank(0)
+        quantise_x_bank(1)
+        quantise_weight(MU, 0)
+        quantise_weight(ALPHA, 0)
+        for step in range(STEPS + LAG):
+            if step < STEPS:
+                density_tile(step)
+            if step + 1 < KT:
+                for w in (SIGMA, MU, ALPHA):
+                    quantise_weight(w, step + 1)
+            next_bank = step // 2 + 2
+            if step % 2 == 0 and next_bank < N_CHUNKS * X_BANKS:
+                quantise_x_bank(next_bank)
+            if step >= LAG:
+                reduce_block(step - LAG)
+
+        log_sum = const.tile([P, 2, D, n_blocks], F32)
+        nc.scalar.activation(out=log_sum[:], in_=exp_sum[:], func=ACT.Ln)
+        lse = const.tile([P, 2, D, n_blocks], F32)
+        nc.vector.tensor_tensor(out=lse[:], in0=log_sum[:], in1=neg_max[:], op=ALU.subtract)
+        per_d = const.tile([P, D, n_blocks], F32)
+        nc.vector.tensor_tensor(out=per_d[:], in0=lse[:, 0], in1=lse[:, 1], op=ALU.subtract)
+        nc.vector.scalar_tensor_tensor(
+            out=result[:, 0:n_blocks],
+            in0=per_d[:, 0, :],
+            scalar=-math.log(2.0 * math.pi),
+            in1=per_d[:, 1, :],
+            op0=ALU.add,
+            op1=ALU.add,
+        )
+        result_bank = tp_psum.tile([P, P], F32, tag="bank")
+        nc.tensor.transpose(out=result_bank[:], in_=result[:], identity=ident_f32[:])
+        out_rows = const.tile([n_blocks, P], F32)
+        nc.scalar.copy(out=out_rows[:], in_=result_bank[0:n_blocks, :])
+        nc.sync.dma_start(out=out.rearrange("(j p) -> j p", p=P), in_=out_rows[:])

@@ -25,7 +25,8 @@ N_CHUNKS = B // N_COLS
 BLOCKS = N_COLS // P
 STEPS = N_CHUNKS * D * KT
 X_BANKS = 2 * D
-LAG = KT + 1
+LAG_T = KT + 3
+LAG_A = KT + 1
 CLIP = 20.0
 SIGMA, MU, ALPHA = 0, 1, 2
 
@@ -43,10 +44,11 @@ def tile_rnadeoutputlayer_t_kernel(
         const = ctx.enter_context(tc.tile_pool(name="const", bufs=1))
         raw = ctx.enter_context(tc.tile_pool(name="raw", bufs=1))
         stage = ctx.enter_context(tc.tile_pool(name="stage", bufs=3))
-        work = ctx.enter_context(tc.tile_pool(name="work", bufs=3))
+        work = ctx.enter_context(tc.tile_pool(name="work", bufs=4))
         keep = ctx.enter_context(tc.tile_pool(name="keep", bufs=3 * KT))
         mx_psum = ctx.enter_context(tc.psum_pool(name="mx_psum", bufs=1))
         tp_psum = ctx.enter_context(tc.psum_pool(name="tp_psum", bufs=5))
+        ctx.enter_context(tc.manual_schedule())
 
         x_rows = x.rearrange("b (t hl) d -> (b t) (hl d)", t=PACK).rearrange(
             "(r p) c -> p r c", p=P
@@ -152,16 +154,21 @@ def tile_rnadeoutputlayer_t_kernel(
             else:
                 nc.scalar.copy(out=grouped_part, in_=bank)
 
-        def quantise_weight(w, kt):
-            v_raw = v_raws[(w, kt)]
+        v_banks = {}
+        x_banks = {}
+
+        def transpose_weight(w, kt):
             bank = tp_psum.tile([P, D, v_tiles_per_kt, P], BF16, tag="bank")
             for d in range(D):
                 for r in range(v_tiles_per_kt):
                     nc.tensor.transpose(
-                        out=bank[:, d, r, :], in_=v_raw[:, r, :, d], identity=ident_bf16[:]
+                        out=bank[:, d, r, :], in_=v_raws[(w, kt)][:, r, :, d], identity=ident_bf16[:]
                     )
+            v_banks[(w, kt)] = bank
+
+        def quantise_weight(w, kt):
             v_grouped = stage.tile([P, BANK_BF16], BF16, align_bytes=64)
-            empty_bank(w, v_grouped[:], bank[:].rearrange("p d r c -> p (d r c)"))
+            empty_bank(w, v_grouped[:], v_banks[(w, kt)][:].rearrange("p d r c -> p (d r c)"))
             nc.vector.quantize_mx(
                 out=v_codes[w][:, kt].rearrange("p d k -> p (d k)").bitcast(FP8X4),
                 scales=v_scales[w][:, kt].rearrange("p d k -> p (d k)"),
@@ -172,149 +179,244 @@ def tile_rnadeoutputlayer_t_kernel(
         x_codes = {}
         x_scales = {}
 
-        def quantise_x_bank(n):
-            chunk, d, half = n // X_BANKS, (n % X_BANKS) // 2, n % 2
-            group = (chunk, d)
+        def x_bank_place(n):
+            return n // X_BANKS, (n % X_BANKS) // 2, n % 2
+
+        def transpose_x_bank(n):
+            chunk, d, half = x_bank_place(n)
             tiles = x_tiles_per_chunk // 2
             bank = tp_psum.tile([P, tiles, P], BF16, tag="bank")
             for r in range(tiles):
                 nc.tensor.transpose(
                     out=bank[:, r, :], in_=x_raws[chunk][:, half * tiles + r, :, d], identity=ident_bf16[:]
                 )
+            x_banks[n] = bank
+
+        def empty_x_bank(n):
+            chunk, d, half = x_bank_place(n)
             if half == 0:
-                x_grouped[group] = stage.tile(
+                x_grouped[(chunk, d)] = stage.tile(
                     [P, 2, BANK_BF16], BF16, name="x_grouped", align_bytes=64
                 )
-            empty_bank(n, x_grouped[group][:, half, :], bank[:].rearrange("p r c -> p (r c)"))
-            if half == 1:
-                x_codes[group] = stage.tile([P, N_COLS], U32, name="x_codes", align_bytes=64)
-                x_scales[group] = stage.tile([P, N_COLS], U8, name="x_scales", align_bytes=64)
-                nc.vector.quantize_mx(
-                    out=x_codes[group][:].bitcast(FP8X4),
-                    scales=x_scales[group][:],
-                    in_=x_grouped[group][:].rearrange("p h c -> p (h c)"),
-                )
+            empty_bank(n, x_grouped[(chunk, d)][:, half, :], x_banks[n][:].rearrange("p r c -> p (r c)"))
 
-        t_tiles = {}
-        a_tiles = {}
+        def quantise_x(g):
+            group = (g // D, g % D)
+            x_codes[group] = stage.tile([P, N_COLS], U32, name="x_codes", align_bytes=64)
+            x_scales[group] = stage.tile([P, N_COLS], U8, name="x_scales", align_bytes=64)
+            nc.vector.quantize_mx(
+                out=x_codes[group][:].bitcast(FP8X4),
+                scales=x_scales[group][:],
+                in_=x_grouped[group][:].rearrange("p h c -> p (h c)"),
+            )
 
-        def product(w, kt, group, tag):
-            acc = mx_psum.tile([P, N_COLS], F32, name="acc_" + tag, tag=tag)
+        acc = {}
+        clipped = {}
+        inv_sigma = {}
+        distance = {}
+        z = {}
+        half_z2 = {}
+        penalty = {}
+        kept = {}
+        turned = {}
+
+        def place(step):
+            return step // (D * KT), (step // KT) % D, step % KT
+
+        def product(w, step):
+            chunk, d, kt = place(step)
+            acc[(w, step)] = mx_psum.tile([P, N_COLS], F32, name="acc%d" % w)
             nc.tensor.matmul_mx(
-                out=acc[:],
-                lhsT=v_codes[w][:, kt, group[1], :].bitcast(FP8X4),
-                lhsT_scale=v_scales[w][:, kt, group[1], :],
-                rhs=x_codes[group][:].bitcast(FP8X4),
-                rhs_scale=x_scales[group][:],
+                out=acc[(w, step)][:],
+                lhsT=v_codes[w][:, kt, d, :].bitcast(FP8X4),
+                lhsT_scale=v_scales[w][:, kt, d, :],
+                rhs=x_codes[(chunk, d)][:].bitcast(FP8X4),
+                rhs_scale=x_scales[(chunk, d)][:],
                 start=True,
                 stop=True,
             )
-            return acc
 
-        def density_tile(step):
-            chunk, d, kt = step // (D * KT), (step // KT) % D, step % KT
-            group = (chunk, d)
-            column = slice(kt, kt + 1)
-
-            sigma_acc = product(SIGMA, kt, group, "sigma")
-            clipped = work.tile([P, N_COLS], F32)
+        def clip_log_sigma(step):
+            chunk, d, kt = place(step)
+            clipped[step] = work.tile([P, N_COLS], F32, name="clipped")
             nc.vector.tensor_scalar(
-                out=clipped[:],
-                in0=sigma_acc[:],
-                scalar1=clip_low[:, d, column],
-                scalar2=clip_high[:, d, column],
+                out=clipped[step][:],
+                in0=acc[(SIGMA, step)][:],
+                scalar1=clip_low[:, d, kt : kt + 1],
+                scalar2=clip_high[:, d, kt : kt + 1],
                 op0=ALU.max,
                 op1=ALU.min,
             )
-            inv_sigma = work.tile([P, N_COLS], F32)
+
+        def exp_minus_log_sigma(step):
+            chunk, d, kt = place(step)
+            inv_sigma[step] = work.tile([P, N_COLS], F32, name="inv_sigma")
             nc.scalar.activation(
-                out=inv_sigma[:], in_=clipped[:], func=ACT.Exp, bias=neg_b_sig[:, d, column], scale=-1.0
+                out=inv_sigma[step][:],
+                in_=clipped[step][:],
+                func=ACT.Exp,
+                bias=neg_b_sig[:, d, kt : kt + 1],
+                scale=-1.0,
             )
 
-            mu_acc = product(MU, kt, group, "mu")
-            distance = work.tile([P, N_COLS], F32)
+        def mu_minus_y(step):
+            chunk, d, kt = place(step)
+            distance[step] = work.tile([P, N_COLS], F32, name="distance")
             nc.vector.scalar_tensor_tensor(
-                out=distance[:],
-                in0=mu_acc[:],
+                out=distance[step][:],
+                in0=acc[(MU, step)][:],
                 scalar=bias[:, d, KT * MU + kt : KT * MU + kt + 1],
                 in1=y_tiles[chunk][:, :, d],
                 op0=ALU.add,
                 op1=ALU.subtract,
             )
-            z = work.tile([P, N_COLS], F32)
-            nc.gpsimd.tensor_tensor(out=z[:], in0=distance[:], in1=inv_sigma[:], op=ALU.mult)
-            half_z2 = work.tile([P, N_COLS], F32)
-            nc.scalar.activation(out=half_z2[:], in_=z[:], func=ACT.Square, scale=math.sqrt(0.5))
-            penalty = work.tile([P, N_COLS], F32)
-            nc.gpsimd.tensor_tensor(out=penalty[:], in0=clipped[:], in1=half_z2[:], op=ALU.add)
 
-            alpha_acc = product(ALPHA, kt, group, "alpha")
-            a_tile = keep.tile([P, N_COLS], F32)
+        def divide_by_sigma(step):
+            z[step] = work.tile([P, N_COLS], F32, name="z")
+            nc.gpsimd.tensor_tensor(
+                out=z[step][:], in0=distance[step][:], in1=inv_sigma[step][:], op=ALU.mult
+            )
+
+        def square(step):
+            half_z2[step] = work.tile([P, N_COLS], F32, name="half_z2")
             nc.scalar.activation(
-                out=a_tile[:],
-                in_=alpha_acc[:],
+                out=half_z2[step][:], in_=z[step][:], func=ACT.Square, scale=math.sqrt(0.5)
+            )
+
+        def add_penalty(step):
+            penalty[step] = work.tile([P, N_COLS], F32, name="penalty")
+            nc.gpsimd.tensor_tensor(
+                out=penalty[step][:], in0=clipped[step][:], in1=half_z2[step][:], op=ALU.add
+            )
+
+        def make_a(step):
+            chunk, d, kt = place(step)
+            kept[(1, step)] = keep.tile([P, N_COLS], F32, name="a_tile")
+            nc.scalar.activation(
+                out=kept[(1, step)][:],
+                in_=acc[(ALPHA, step)][:],
                 func=ACT.Identity,
                 bias=bias[:, d, KT * ALPHA + kt : KT * ALPHA + kt + 1],
                 scale=1.0,
             )
-            t_tile = keep.tile([P, N_COLS], F32)
+
+        def make_t(step):
+            chunk, d, kt = place(step)
+            kept[(0, step)] = keep.tile([P, N_COLS], F32, name="t_tile")
             nc.vector.scalar_tensor_tensor(
-                out=t_tile[:],
-                in0=a_tile[:],
-                scalar=neg_b_sig[:, d, column],
-                in1=penalty[:],
+                out=kept[(0, step)][:],
+                in0=kept[(1, step)][:],
+                scalar=neg_b_sig[:, d, kt : kt + 1],
+                in1=penalty[step][:],
                 op0=ALU.add,
                 op1=ALU.subtract,
             )
-            t_tiles[step] = t_tile
-            a_tiles[step] = a_tile
 
-        def reduce_block(block):
-            first_step = (block // BLOCKS) * KT
+        def statistic(tile_, kind, block):
             chunk, d, j = block // (D * BLOCKS), (block // BLOCKS) % D, block % BLOCKS
             column = chunk * BLOCKS + j
-            samples = slice(j * P, (j + 1) * P)
-            for kind, tiles in enumerate((t_tiles, a_tiles)):
-                turned = tp_psum.tile([P, K], F32, tag="bank")
-                for kt in range(KT):
-                    nc.tensor.transpose(
-                        out=turned[:, kt * P : (kt + 1) * P],
-                        in_=tiles[first_step + kt][:, samples],
-                        identity=ident_f32[:],
-                    )
-                nc.vector.tensor_reduce(
-                    out=neg_max[:, kind, d, column : column + 1],
-                    in_=turned[:],
-                    axis=AXIS.X,
-                    op=ALU.max,
-                    negate=True,
-                )
-                unread = work.tile([P, K], F32)
-                nc.scalar.activation(
-                    out=unread[:],
-                    in_=turned[:],
-                    func=ACT.Exp,
-                    bias=neg_max[:, kind, d, column : column + 1],
-                    scale=1.0,
-                    accum_out=exp_sum[:, kind, d, column : column + 1],
+            return tile_[:, kind, d, column : column + 1]
+
+        def turn(kind, block):
+            first_step = (block // BLOCKS) * KT
+            j = block % BLOCKS
+            turned[(kind, block)] = tp_psum.tile([P, K], F32, name="turned", tag="bank")
+            for kt in range(KT):
+                nc.tensor.transpose(
+                    out=turned[(kind, block)][:, kt * P : (kt + 1) * P],
+                    in_=kept[(kind, first_step + kt)][:, j * P : (j + 1) * P],
+                    identity=ident_f32[:],
                 )
 
-        quantise_weight(SIGMA, 0)
-        quantise_x_bank(0)
-        quantise_x_bank(1)
-        quantise_weight(MU, 0)
-        quantise_weight(ALPHA, 0)
-        for step in range(STEPS + LAG):
-            if step < STEPS:
-                density_tile(step)
-            if step + 1 < KT:
+        def maximum(kind, block):
+            nc.vector.tensor_reduce(
+                out=statistic(neg_max, kind, block),
+                in_=turned[(kind, block)][:],
+                axis=AXIS.X,
+                op=ALU.max,
+                negate=True,
+            )
+
+        def sum_of_exp(kind, block):
+            unread = work.tile([P, K], F32)
+            nc.scalar.activation(
+                out=unread[:],
+                in_=turned[(kind, block)][:],
+                func=ACT.Exp,
+                bias=statistic(neg_max, kind, block),
+                scale=1.0,
+                accum_out=statistic(exp_sum, kind, block),
+            )
+
+        n_x_banks = N_CHUNKS * X_BANKS
+
+        def is_step(step):
+            return 0 <= step < STEPS
+
+        def is_block(block):
+            return 0 <= block < STEPS
+
+        for i in range(-2, STEPS + LAG_T + 2):
+            if is_block(i - LAG_T):
+                turn(0, i - LAG_T)
+            if is_block(i - LAG_A):
+                turn(1, i - LAG_A)
+            if is_step(i - 2):
+                square(i - 2)
+            if is_step(i - 1):
+                make_a(i - 1)
+            if is_step(i):
+                clip_log_sigma(i)
+                mu_minus_y(i)
+
+            if i == -1:
+                quantise_weight(SIGMA, 0)
+                empty_x_bank(0)
+                empty_x_bank(1)
+                quantise_x(0)
+                quantise_weight(MU, 0)
+                quantise_weight(ALPHA, 0)
+            elif 0 <= i < KT - 1:
                 for w in (SIGMA, MU, ALPHA):
-                    quantise_weight(w, step + 1)
-            next_bank = step // 2 + 2
-            if step % 2 == 0 and next_bank < N_CHUNKS * X_BANKS:
-                quantise_x_bank(next_bank)
-            if step >= LAG:
-                reduce_block(step - LAG)
+                    quantise_weight(w, i + 1)
+            if i % 2 == 0 and 2 <= (i + 4) // 2 < n_x_banks:
+                empty_x_bank((i + 4) // 2)
+
+            if is_step(i + 1):
+                product(SIGMA, i + 1)
+                product(MU, i + 1)
+            if is_step(i):
+                product(ALPHA, i)
+            if is_step(i - 1):
+                divide_by_sigma(i - 1)
+            if is_step(i - 2):
+                add_penalty(i - 2)
+            if is_step(i - 3):
+                make_t(i - 3)
+            if is_block(i - LAG_T):
+                maximum(0, i - LAG_T)
+            if is_block(i - LAG_A):
+                maximum(1, i - LAG_A)
+            if i % 4 == 2 and 1 <= (i + 2) // 4 < N_CHUNKS * D:
+                quantise_x((i + 2) // 4)
+            if is_block(i - LAG_T - 1):
+                sum_of_exp(0, i - LAG_T - 1)
+            if is_block(i - LAG_A - 1):
+                sum_of_exp(1, i - LAG_A - 1)
+            if is_step(i):
+                exp_minus_log_sigma(i)
+
+            if i == -2:
+                transpose_weight(SIGMA, 0)
+                transpose_x_bank(0)
+                transpose_x_bank(1)
+                transpose_weight(MU, 0)
+                transpose_weight(ALPHA, 0)
+            elif i + 2 < KT:
+                for w in (SIGMA, MU, ALPHA):
+                    transpose_weight(w, i + 2)
+            if i % 2 == 1 and 2 <= (i + 5) // 2 < n_x_banks:
+                transpose_x_bank((i + 5) // 2)
 
         log_sum = const.tile([P, 2, D, n_blocks], F32)
         nc.scalar.activation(out=log_sum[:], in_=exp_sum[:], func=ACT.Ln)

@@ -137,6 +137,11 @@ def tile_rnadeoutputlayer_t_kernel(
             out=clip_high[:], in0=b_sig, scalar1=-1.0, scalar2=CLIP, op0=ALU.mult, op1=ALU.add
         )
 
+        b_alp_sig = const.tile([P, D, KT], F32)
+        nc.vector.tensor_tensor(
+            out=b_alp_sig[:], in0=bias[:, :, KT * ALPHA : KT * (ALPHA + 1)], in1=b_sig, op=ALU.subtract
+        )
+
         n_blocks = B // P
         neg_max = const.tile([P, 2, D, n_blocks], F32)
         exp_sum = const.tile([P, 2, D, n_blocks], F32)
@@ -223,11 +228,11 @@ def tile_rnadeoutputlayer_t_kernel(
         def place(step):
             return step // (D * KT), (step // KT) % D, step % KT
 
-        def product(w, step):
+        def product(w, step, use=""):
             chunk, d, kt = place(step)
-            acc[(w, step)] = mx_psum.tile([P, N_COLS], F32, name="acc%d" % w)
+            acc[(w, step, use)] = mx_psum.tile([P, N_COLS], F32, name="acc%d" % w)
             nc.tensor.matmul_mx(
-                out=acc[(w, step)][:],
+                out=acc[(w, step, use)][:],
                 lhsT=v_codes[w][:, kt, d, :].bitcast(FP8X4),
                 lhsT_scale=v_scales[w][:, kt, d, :],
                 rhs=x_codes[(chunk, d)][:].bitcast(FP8X4),
@@ -241,7 +246,7 @@ def tile_rnadeoutputlayer_t_kernel(
             clipped[step] = work.tile([P, N_COLS], F32, name="clipped")
             nc.vector.tensor_scalar(
                 out=clipped[step][:],
-                in0=acc[(SIGMA, step)][:],
+                in0=acc[(SIGMA, step, "")][:],
                 scalar1=clip_low[:, d, kt : kt + 1],
                 scalar2=clip_high[:, d, kt : kt + 1],
                 op0=ALU.max,
@@ -264,7 +269,7 @@ def tile_rnadeoutputlayer_t_kernel(
             distance[step] = work.tile([P, N_COLS], F32, name="distance")
             nc.vector.scalar_tensor_tensor(
                 out=distance[step][:],
-                in0=acc[(MU, step)][:],
+                in0=acc[(MU, step, "")][:],
                 scalar=bias[:, d, KT * MU + kt : KT * MU + kt + 1],
                 in1=y_tiles[chunk][:, :, d],
                 op0=ALU.add,
@@ -294,7 +299,7 @@ def tile_rnadeoutputlayer_t_kernel(
             kept[(1, step)] = keep.tile([P, N_COLS], F32, name="a_tile")
             nc.scalar.activation(
                 out=kept[(1, step)][:],
-                in_=acc[(ALPHA, step)][:],
+                in_=acc[(ALPHA, step, "a")][:],
                 func=ACT.Identity,
                 bias=bias[:, d, KT * ALPHA + kt : KT * ALPHA + kt + 1],
                 scale=1.0,
@@ -305,8 +310,8 @@ def tile_rnadeoutputlayer_t_kernel(
             kept[(0, step)] = keep.tile([P, N_COLS], F32, name="t_tile")
             nc.vector.scalar_tensor_tensor(
                 out=kept[(0, step)][:],
-                in0=kept[(1, step)][:],
-                scalar=neg_b_sig[:, d, kt : kt + 1],
+                in0=acc[(ALPHA, step, "t")][:],
+                scalar=b_alp_sig[:, d, kt : kt + 1],
                 in1=penalty[step][:],
                 op0=ALU.add,
                 op1=ALU.subtract,
@@ -385,26 +390,14 @@ def tile_rnadeoutputlayer_t_kernel(
             if is_step(i + 1):
                 product(SIGMA, i + 1)
                 product(MU, i + 1)
-            if is_step(i):
-                product(ALPHA, i)
+            if is_step(i - 3):
+                product(ALPHA, i - 3, "t")
             if is_step(i - 1):
                 divide_by_sigma(i - 1)
             if is_step(i - 2):
                 add_penalty(i - 2)
             if is_step(i - 3):
                 make_t(i - 3)
-            if is_block(i - LAG_T):
-                maximum(0, i - LAG_T)
-            if is_block(i - LAG_A):
-                maximum(1, i - LAG_A)
-            if i % 4 == 2 and 1 <= (i + 2) // 4 < N_CHUNKS * D:
-                quantise_x((i + 2) // 4)
-            if is_block(i - LAG_T - 1):
-                sum_of_exp(0, i - LAG_T - 1)
-            if is_block(i - LAG_A - 1):
-                sum_of_exp(1, i - LAG_A - 1)
-            if is_step(i):
-                exp_minus_log_sigma(i)
 
             if i == -2:
                 transpose_weight(SIGMA, 0)
@@ -417,6 +410,21 @@ def tile_rnadeoutputlayer_t_kernel(
                     transpose_weight(w, i + 2)
             if i % 2 == 1 and 2 <= (i + 5) // 2 < n_x_banks:
                 transpose_x_bank((i + 5) // 2)
+            if is_step(i):
+                product(ALPHA, i, "a")
+
+            if is_block(i - LAG_T):
+                maximum(0, i - LAG_T)
+            if is_block(i - LAG_A):
+                maximum(1, i - LAG_A)
+            if i % 4 == 2 and 1 <= (i + 2) // 4 < N_CHUNKS * D:
+                quantise_x((i + 2) // 4)
+            if is_block(i - LAG_T - 1):
+                sum_of_exp(0, i - LAG_T - 1)
+            if is_block(i - LAG_A - 1):
+                sum_of_exp(1, i - LAG_A - 1)
+            if is_step(i):
+                exp_minus_log_sigma(i)
 
         log_sum = const.tile([P, 2, D, n_blocks], F32)
         nc.scalar.activation(out=log_sum[:], in_=exp_sum[:], func=ACT.Ln)

@@ -47,7 +47,7 @@ def tile_rnadeoutputlayer_t_kernel(
         work = ctx.enter_context(tc.tile_pool(name="work", bufs=4))
         keep = ctx.enter_context(tc.tile_pool(name="keep", bufs=3 * KT))
         mx_psum = ctx.enter_context(tc.psum_pool(name="mx_psum", bufs=1))
-        tp_psum = ctx.enter_context(tc.psum_pool(name="tp_psum", bufs=5))
+        tp_psum = ctx.enter_context(tc.psum_pool(name="tp_psum", bufs=4))
         ctx.enter_context(tc.manual_schedule())
 
         x_rows = x.rearrange("b (t hl) d -> (b t) (hl d)", t=PACK).rearrange(
@@ -230,7 +230,7 @@ def tile_rnadeoutputlayer_t_kernel(
 
         def product(w, step, use=""):
             chunk, d, kt = place(step)
-            acc[(w, step, use)] = mx_psum.tile([P, N_COLS], F32, name="acc%d" % w)
+            acc[(w, step, use)] = mx_psum.tile([P, N_COLS], F32, name="acc%d%s" % (w, use))
             nc.tensor.matmul_mx(
                 out=acc[(w, step, use)][:],
                 lhsT=v_codes[w][:, kt, d, :].bitcast(FP8X4),
@@ -387,31 +387,19 @@ def tile_rnadeoutputlayer_t_kernel(
             if i % 2 == 0 and 2 <= (i + 4) // 2 < n_x_banks:
                 empty_x_bank((i + 4) // 2)
 
+            if is_step(i - 3):
+                make_t(i - 3)
             if is_step(i + 1):
                 product(SIGMA, i + 1)
                 product(MU, i + 1)
-            if is_step(i - 3):
-                product(ALPHA, i - 3, "t")
+            if is_step(i):
+                product(ALPHA, i, "a")
+            if is_step(i - 2):
+                product(ALPHA, i - 2, "t")
             if is_step(i - 1):
                 divide_by_sigma(i - 1)
             if is_step(i - 2):
                 add_penalty(i - 2)
-            if is_step(i - 3):
-                make_t(i - 3)
-
-            if i == -2:
-                transpose_weight(SIGMA, 0)
-                transpose_x_bank(0)
-                transpose_x_bank(1)
-                transpose_weight(MU, 0)
-                transpose_weight(ALPHA, 0)
-            elif i + 2 < KT:
-                for w in (SIGMA, MU, ALPHA):
-                    transpose_weight(w, i + 2)
-            if i % 2 == 1 and 2 <= (i + 5) // 2 < n_x_banks:
-                transpose_x_bank((i + 5) // 2)
-            if is_step(i):
-                product(ALPHA, i, "a")
 
             if is_block(i - LAG_T):
                 maximum(0, i - LAG_T)
@@ -425,6 +413,18 @@ def tile_rnadeoutputlayer_t_kernel(
                 sum_of_exp(1, i - LAG_A - 1)
             if is_step(i):
                 exp_minus_log_sigma(i)
+
+            if i == -2:
+                transpose_weight(SIGMA, 0)
+                transpose_x_bank(0)
+                transpose_x_bank(1)
+                transpose_weight(MU, 0)
+                transpose_weight(ALPHA, 0)
+            elif i + 2 < KT:
+                for w in (SIGMA, MU, ALPHA):
+                    transpose_weight(w, i + 2)
+            if i % 2 == 1 and 2 <= (i + 5) // 2 < n_x_banks:
+                transpose_x_bank((i + 5) // 2)
 
         log_sum = const.tile([P, 2, D, n_blocks], F32)
         nc.scalar.activation(out=log_sum[:], in_=exp_sum[:], func=ACT.Ln)

@@ -7,6 +7,7 @@ from concourse.masks import make_identity
 F32 = mybir.dt.float32
 BF16 = mybir.dt.bfloat16
 U32 = mybir.dt.uint32
+I32 = mybir.dt.int32
 U8 = mybir.dt.uint8
 FP8X4 = mybir.dt.float8_e4m3fn_x4
 ALU = mybir.AluOpType
@@ -80,11 +81,8 @@ def tile_rnadeoutputlayer_t_kernel(
 
         v_raws = {}
         x_raws = {}
-        v_raws[(SIGMA, 0)] = load_weight(SIGMA, 0)
         x_raws[0] = load_x(0)
-        v_raws[(MU, 0)] = load_weight(MU, 0)
-        v_raws[(ALPHA, 0)] = load_weight(ALPHA, 0)
-        for kt in range(1, KT):
+        for kt in range(KT):
             for w in (SIGMA, MU, ALPHA):
                 v_raws[(w, kt)] = load_weight(w, kt)
         for chunk in range(1, N_CHUNKS):
@@ -97,21 +95,17 @@ def tile_rnadeoutputlayer_t_kernel(
                 out=bias_rows[KT * w : KT * (w + 1)].rearrange("kt kl d -> kt (kl d)"),
                 in_=biases[w].rearrange("(kt kl) d -> kt (kl d)", kt=KT),
             )
-        y_tiles = []
-        for chunk in range(N_CHUNKS):
-            y_all = const.tile([P, N_COLS, D], BF16, name="y_all%d" % chunk)
-            nc.scalar.dma_start(
-                out=y_all[:].rearrange("p b d -> p (b d)"),
-                in_=input_var[chunk * N_COLS : (chunk + 1) * N_COLS, :]
-                .rearrange("b d -> (b d)")
-                .partition_broadcast(P),
-            )
-            y_tiles.append(y_all)
+        y_row = const.tile([P, B * D], BF16)
+        nc.vector.memset(y_row[:].bitcast(I32), 0)
+        nc.scalar.dma_start(out=y_row[0:1, :], in_=input_var.rearrange("(o b) d -> o (b d)", o=1))
 
         ident_bf16 = const.tile([P, P], BF16)
         make_identity(nc, ident_bf16[:])
         ident_f32 = const.tile([P, P], F32)
         make_identity(nc, ident_f32[:])
+
+        ones = const.tile([P, P], BF16)
+        nc.vector.memset(ones[:], 1.0)
 
         warm = const.tile([P, 2], F32)
         nc.vector.memset(warm[:], 0.0)
@@ -120,27 +114,34 @@ def tile_rnadeoutputlayer_t_kernel(
         result = const.tile([P, P], F32)
         nc.vector.memset(result[:], 0.0)
 
-        bias_bank = tp_psum.tile([P, D, P], BF16, tag="bank")
-        for d in range(D):
-            nc.tensor.transpose(out=bias_bank[:, d, :], in_=bias_rows[:, :, d], identity=ident_bf16[:])
         bias = const.tile([P, D, 3 * KT], F32)
-        nc.vector.tensor_copy(out=bias[:], in_=bias_bank[:, :, 0 : 3 * KT])
-        b_sig = bias[:, :, KT * SIGMA : KT * (SIGMA + 1)]
         neg_b_sig = const.tile([P, D, KT], F32)
-        nc.vector.tensor_scalar(out=neg_b_sig[:], in0=b_sig, scalar1=-1.0, scalar2=None, op0=ALU.mult)
         clip_low = const.tile([P, D, KT], F32)
-        nc.vector.tensor_scalar(
-            out=clip_low[:], in0=b_sig, scalar1=-1.0, scalar2=-CLIP, op0=ALU.mult, op1=ALU.add
-        )
         clip_high = const.tile([P, D, KT], F32)
-        nc.vector.tensor_scalar(
-            out=clip_high[:], in0=b_sig, scalar1=-1.0, scalar2=CLIP, op0=ALU.mult, op1=ALU.add
-        )
-
         b_alp_sig = const.tile([P, D, KT], F32)
-        nc.vector.tensor_tensor(
-            out=b_alp_sig[:], in0=bias[:, :, KT * ALPHA : KT * (ALPHA + 1)], in1=b_sig, op=ALU.subtract
-        )
+        bias_banks = {}
+
+        def transpose_biases():
+            bias_banks[0] = tp_psum.tile([P, D, P], BF16, name="bias_bank", tag="bank")
+            for d in range(D):
+                nc.tensor.transpose(
+                    out=bias_banks[0][:, d, :], in_=bias_rows[:, :, d], identity=ident_bf16[:]
+                )
+
+        def bias_columns():
+            nc.vector.tensor_copy(out=bias[:], in_=bias_banks[0][:, :, 0 : 3 * KT])
+            b_sig = bias[:, :, KT * SIGMA : KT * (SIGMA + 1)]
+            b_alp = bias[:, :, KT * ALPHA : KT * (ALPHA + 1)]
+            nc.vector.tensor_scalar(
+                out=neg_b_sig[:], in0=b_sig, scalar1=-1.0, scalar2=None, op0=ALU.mult
+            )
+            nc.vector.tensor_scalar(
+                out=clip_low[:], in0=b_sig, scalar1=-1.0, scalar2=-CLIP, op0=ALU.mult, op1=ALU.add
+            )
+            nc.vector.tensor_scalar(
+                out=clip_high[:], in0=b_sig, scalar1=-1.0, scalar2=CLIP, op0=ALU.mult, op1=ALU.add
+            )
+            nc.vector.tensor_tensor(out=b_alp_sig[:], in0=b_alp, in1=b_sig, op=ALU.subtract)
 
         n_blocks = B // P
         neg_max = const.tile([P, 2, D, n_blocks], F32)
@@ -158,6 +159,30 @@ def tile_rnadeoutputlayer_t_kernel(
                 nc.vector.tensor_copy(out=grouped_part, in_=bank)
             else:
                 nc.scalar.copy(out=grouped_part, in_=bank)
+
+        y_banks = {}
+        y_all = [const.tile([P, D, N_COLS], BF16, name="y_all%d" % chunk) for chunk in range(N_CHUNKS)]
+
+        def spread_y(chunk):
+            for half in range(2):
+                first = (2 * chunk + half) * N_COLS
+                y_banks[(chunk, half)] = tp_psum.tile([P, N_COLS], F32, name="y_bank", tag="bank")
+                nc.tensor.matmul(
+                    out=y_banks[(chunk, half)][:],
+                    lhsT=ones[:],
+                    rhs=y_row[:, first : first + N_COLS],
+                    start=True,
+                    stop=True,
+                )
+
+        def keep_y(chunk):
+            samples = N_COLS // D
+            for half in range(2):
+                empty_bank(
+                    half,
+                    y_all[chunk][:, :, half * samples : (half + 1) * samples],
+                    y_banks[(chunk, half)][:].rearrange("p (b d) -> p d b", d=D),
+                )
 
         v_banks = {}
         x_banks = {}
@@ -271,7 +296,7 @@ def tile_rnadeoutputlayer_t_kernel(
                 out=distance[step][:],
                 in0=acc[(MU, step, "")][:],
                 scalar=bias[:, d, KT * MU + kt : KT * MU + kt + 1],
-                in1=y_tiles[chunk][:, :, d],
+                in1=y_all[chunk][:, d, :],
                 op0=ALU.add,
                 op1=ALU.subtract,
             )
@@ -361,7 +386,28 @@ def tile_rnadeoutputlayer_t_kernel(
         def is_block(block):
             return 0 <= block < STEPS
 
-        for i in range(-2, STEPS + LAG_T + 2):
+        transpose_x_bank(0)
+        transpose_x_bank(1)
+        transpose_weight(SIGMA, 0)
+        transpose_biases()
+        empty_x_bank(0)
+        empty_x_bank(1)
+        quantise_weight(SIGMA, 0)
+        quantise_x(0)
+        bias_columns()
+        transpose_weight(MU, 0)
+        spread_y(0)
+        quantise_weight(MU, 0)
+        keep_y(0)
+        product(SIGMA, 0)
+        product(MU, 0)
+        transpose_weight(ALPHA, 0)
+        quantise_weight(ALPHA, 0)
+        for w in (SIGMA, MU, ALPHA):
+            transpose_weight(w, 1)
+        transpose_x_bank(2)
+
+        for i in range(STEPS + LAG_T + 2):
             if is_block(i - LAG_T):
                 turn(0, i - LAG_T)
             if is_block(i - LAG_A):
@@ -374,18 +420,13 @@ def tile_rnadeoutputlayer_t_kernel(
                 clip_log_sigma(i)
                 mu_minus_y(i)
 
-            if i == -1:
-                quantise_weight(SIGMA, 0)
-                empty_x_bank(0)
-                empty_x_bank(1)
-                quantise_x(0)
-                quantise_weight(MU, 0)
-                quantise_weight(ALPHA, 0)
-            elif 0 <= i < KT - 1:
+            if i + 1 < KT:
                 for w in (SIGMA, MU, ALPHA):
                     quantise_weight(w, i + 1)
-            if i % 2 == 0 and 2 <= (i + 4) // 2 < n_x_banks:
+            if i % 2 == 0 and (i + 4) // 2 < n_x_banks:
                 empty_x_bank((i + 4) // 2)
+            if 1 <= i - 2 < N_CHUNKS:
+                keep_y(i - 2)
 
             if is_step(i - 3):
                 make_t(i - 3)
@@ -414,17 +455,13 @@ def tile_rnadeoutputlayer_t_kernel(
             if is_step(i):
                 exp_minus_log_sigma(i)
 
-            if i == -2:
-                transpose_weight(SIGMA, 0)
-                transpose_x_bank(0)
-                transpose_x_bank(1)
-                transpose_weight(MU, 0)
-                transpose_weight(ALPHA, 0)
-            elif i + 2 < KT:
+            if i + 2 < KT:
                 for w in (SIGMA, MU, ALPHA):
                     transpose_weight(w, i + 2)
-            if i % 2 == 1 and 2 <= (i + 5) // 2 < n_x_banks:
+            if i % 2 == 1 and (i + 5) // 2 < n_x_banks:
                 transpose_x_bank((i + 5) // 2)
+            if 1 <= i - 1 < N_CHUNKS:
+                spread_y(i - 1)
 
         log_sum = const.tile([P, 2, D, n_blocks], F32)
         nc.scalar.activation(out=log_sum[:], in_=exp_sum[:], func=ACT.Ln)

import math
from contextlib import ExitStack

import concourse.mybir as mybir
from concourse.masks import make_identity

F32 = mybir.dt.float32
BF16 = mybir.dt.bfloat16
U32 = mybir.dt.uint32
I32 = mybir.dt.int32
U8 = mybir.dt.uint8
FP8X4 = mybir.dt.float8_e4m3fn_x4
ALU = mybir.AluOpType
ACT = mybir.ActivationFunctionType
AXIS = mybir.AxisListType

P = 128
PACK = 4
B, K, H, D = 2048, 512, 512, 2
H_LOW = H // PACK
ROWS = P // PACK
N_COLS = 512
BANK_BF16 = 1024
KT = K // P
N_CHUNKS = B // N_COLS
BLOCKS = N_COLS // P
STEPS = N_CHUNKS * D * KT
X_BANKS = 2 * D
LAG_T = KT + 3
LAG_A = KT + 1
CLIP = 20.0
SIGMA, MU, ALPHA = 0, 1, 2

FLOPS = 2 * B * K * H * D * 3


def tile_rnadeoutputlayer_t_kernel(
    tc, x, input_var, V_alpha, V_mu, V_sigma, b_alpha, b_mu, b_sigma, out
):
    nc = tc.nc
    weights = (V_sigma, V_mu, V_alpha)
    biases = (b_sigma, b_mu, b_alpha)

    with ExitStack() as ctx:
        const = ctx.enter_context(tc.tile_pool(name="const", bufs=1))
        raw = ctx.enter_context(tc.tile_pool(name="raw", bufs=1))
        stage = ctx.enter_context(tc.tile_pool(name="stage", bufs=3))
        work = ctx.enter_context(tc.tile_pool(name="work", bufs=4))
        keep = ctx.enter_context(tc.tile_pool(name="keep", bufs=3 * KT))
        mx_psum = ctx.enter_context(tc.psum_pool(name="mx_psum", bufs=1))
        tp_psum = ctx.enter_context(tc.psum_pool(name="tp_psum", bufs=4))
        ctx.enter_context(tc.manual_schedule())

        x_rows = x.rearrange("b (t hl) d -> (b t) (hl d)", t=PACK).rearrange(
            "(r p) c -> p r c", p=P
        )
        x_tiles_per_chunk = N_COLS // ROWS
        v_tiles_per_kt = P // ROWS

        def load_x(chunk):
            x_raw = raw.tile([P, x_tiles_per_chunk, H_LOW, D], BF16, name="x_raw%d" % chunk)
            half = x_tiles_per_chunk // 2
            for part in range(2):
                first = chunk * x_tiles_per_chunk + part * half
                nc.sync.dma_start(
                    out=x_raw[:, part * half : (part + 1) * half].rearrange("p r hl d -> p r (hl d)"),
                    in_=x_rows[:, first : first + half, :],
                )
            return x_raw

        def load_weight(w, kt):
            v_rows = weights[w].rearrange("k (t hl) d -> (k t) (hl d)", t=PACK).rearrange(
                "(r p) c -> p r c", p=P
            )
            v_raw = raw.tile([P, v_tiles_per_kt, H_LOW, D], BF16, name="v_raw%d_%d" % (w, kt))
            nc.sync.dma_start(
                out=v_raw[:].rearrange("p r hl d -> p r (hl d)"),
                in_=v_rows[:, kt * v_tiles_per_kt : (kt + 1) * v_tiles_per_kt, :],
            )
            return v_raw

        v_raws = {}
        x_raws = {}
        x_raws[0] = load_x(0)
        for kt in range(KT):
            for w in (SIGMA, MU, ALPHA):
                v_raws[(w, kt)] = load_weight(w, kt)
        for chunk in range(1, N_CHUNKS):
            x_raws[chunk] = load_x(chunk)

        bias_rows = const.tile([P, P, D], BF16)
        nc.vector.memset(bias_rows[:], 0.0)
        for w in (SIGMA, MU, ALPHA):
            nc.scalar.dma_start(
                out=bias_rows[KT * w : KT * (w + 1)].rearrange("kt kl d -> kt (kl d)"),
                in_=biases[w].rearrange("(kt kl) d -> kt (kl d)", kt=KT),
            )
        y_row = const.tile([P, B * D], BF16)
        nc.vector.memset(y_row[:].bitcast(I32), 0)
        nc.scalar.dma_start(out=y_row[0:1, :], in_=input_var.rearrange("(o b) d -> o (b d)", o=1))

        ident_bf16 = const.tile([P, P], BF16)
        make_identity(nc, ident_bf16[:])
        ident_f32 = const.tile([P, P], F32)
        make_identity(nc, ident_f32[:])

        ones = const.tile([P, P], BF16)
        nc.vector.memset(ones[:], 1.0)

        warm = const.tile([P, 2], F32)
        nc.vector.memset(warm[:], 0.0)
        nc.scalar.activation(out=warm[:, 1:2], in_=warm[:, 0:1], func=ACT.Exp)

        result = const.tile([P, P], F32)
        nc.vector.memset(result[:], 0.0)

        bias = const.tile([P, D, 3 * KT], F32)
        neg_b_sig = const.tile([P, D, KT], F32)
        clip_low = const.tile([P, D, KT], F32)
        clip_high = const.tile([P, D, KT], F32)
        b_alp_sig = const.tile([P, D, KT], F32)
        bias_banks = {}

        def transpose_biases():
            bias_banks[0] = tp_psum.tile([P, D, P], BF16, name="bias_bank", tag="bank")
            for d in range(D):
                nc.tensor.transpose(
                    out=bias_banks[0][:, d, :], in_=bias_rows[:, :, d], identity=ident_bf16[:]
                )

        def bias_columns():
            nc.vector.tensor_copy(out=bias[:], in_=bias_banks[0][:, :, 0 : 3 * KT])
            b_sig = bias[:, :, KT * SIGMA : KT * (SIGMA + 1)]
            b_alp = bias[:, :, KT * ALPHA : KT * (ALPHA + 1)]
            nc.vector.tensor_scalar(
                out=neg_b_sig[:], in0=b_sig, scalar1=-1.0, scalar2=None, op0=ALU.mult
            )
            nc.vector.tensor_scalar(
                out=clip_low[:], in0=b_sig, scalar1=-1.0, scalar2=-CLIP, op0=ALU.mult, op1=ALU.add
            )
            nc.vector.tensor_scalar(
                out=clip_high[:], in0=b_sig, scalar1=-1.0, scalar2=CLIP, op0=ALU.mult, op1=ALU.add
            )
            nc.vector.tensor_tensor(out=b_alp_sig[:], in0=b_alp, in1=b_sig, op=ALU.subtract)

        n_blocks = B // P
        neg_max = const.tile([P, 2, D, n_blocks], F32)
        exp_sum = const.tile([P, 2, D, n_blocks], F32)

        v_codes = [
            const.tile([P, KT, D, P], U32, name="v_codes%d" % w, align_bytes=64) for w in range(3)
        ]
        v_scales = [
            const.tile([P, KT, D, P], U8, name="v_scales%d" % w, align_bytes=64) for w in range(3)
        ]

        def empty_bank(n, grouped_part, bank):
            if n % 2 == 0:
                nc.vector.tensor_copy(out=grouped_part, in_=bank)
            else:
                nc.scalar.copy(out=grouped_part, in_=bank)

        y_banks = {}
        y_all = [const.tile([P, D, N_COLS], BF16, name="y_all%d" % chunk) for chunk in range(N_CHUNKS)]

        def spread_y(chunk):
            for half in range(2):
                first = (2 * chunk + half) * N_COLS
                y_banks[(chunk, half)] = tp_psum.tile([P, N_COLS], F32, name="y_bank", tag="bank")
                nc.tensor.matmul(
                    out=y_banks[(chunk, half)][:],
                    lhsT=ones[:],
                    rhs=y_row[:, first : first + N_COLS],
                    start=True,
                    stop=True,
                )

        def keep_y(chunk):
            samples = N_COLS // D
            for half in range(2):
                empty_bank(
                    half,
                    y_all[chunk][:, :, half * samples : (half + 1) * samples],
                    y_banks[(chunk, half)][:].rearrange("p (b d) -> p d b", d=D),
                )

        v_banks = {}
        x_banks = {}

        def transpose_weight(w, kt):
            bank = tp_psum.tile([P, D, v_tiles_per_kt, P], BF16, tag="bank")
            for d in range(D):
                for r in range(v_tiles_per_kt):
                    nc.tensor.transpose(
                        out=bank[:, d, r, :], in_=v_raws[(w, kt)][:, r, :, d], identity=ident_bf16[:]
                    )
            v_banks[(w, kt)] = bank

        def quantise_weight(w, kt):
            v_grouped = stage.tile([P, BANK_BF16], BF16, align_bytes=64)
            empty_bank(w, v_grouped[:], v_banks[(w, kt)][:].rearrange("p d r c -> p (d r c)"))
            nc.vector.quantize_mx(
                out=v_codes[w][:, kt].rearrange("p d k -> p (d k)").bitcast(FP8X4),
                scales=v_scales[w][:, kt].rearrange("p d k -> p (d k)"),
                in_=v_grouped[:],
            )

        x_grouped = {}
        x_codes = {}
        x_scales = {}

        def x_bank_place(n):
            return n // X_BANKS, (n % X_BANKS) // 2, n % 2

        def transpose_x_bank(n):
            chunk, d, half = x_bank_place(n)
            tiles = x_tiles_per_chunk // 2
            bank = tp_psum.tile([P, tiles, P], BF16, tag="bank")
            for r in range(tiles):
                nc.tensor.transpose(
                    out=bank[:, r, :], in_=x_raws[chunk][:, half * tiles + r, :, d], identity=ident_bf16[:]
                )
            x_banks[n] = bank

        def empty_x_bank(n):
            chunk, d, half = x_bank_place(n)
            if half == 0:
                x_grouped[(chunk, d)] = stage.tile(
                    [P, 2, BANK_BF16], BF16, name="x_grouped", align_bytes=64
                )
            empty_bank(n, x_grouped[(chunk, d)][:, half, :], x_banks[n][:].rearrange("p r c -> p (r c)"))

        def quantise_x(g):
            group = (g // D, g % D)
            x_codes[group] = stage.tile([P, N_COLS], U32, name="x_codes", align_bytes=64)
            x_scales[group] = stage.tile([P, N_COLS], U8, name="x_scales", align_bytes=64)
            nc.vector.quantize_mx(
                out=x_codes[group][:].bitcast(FP8X4),
                scales=x_scales[group][:],
                in_=x_grouped[group][:].rearrange("p h c -> p (h c)"),
            )

        acc = {}
        clipped = {}
        inv_sigma = {}
        distance = {}
        z = {}
        half_z2 = {}
        penalty = {}
        kept = {}
        turned = {}

        def place(step):
            return step // (D * KT), (step // KT) % D, step % KT

        def product(w, step, use=""):
            chunk, d, kt = place(step)
            acc[(w, step, use)] = mx_psum.tile([P, N_COLS], F32, name="acc%d%s" % (w, use))
            nc.tensor.matmul_mx(
                out=acc[(w, step, use)][:],
                lhsT=v_codes[w][:, kt, d, :].bitcast(FP8X4),
                lhsT_scale=v_scales[w][:, kt, d, :],
                rhs=x_codes[(chunk, d)][:].bitcast(FP8X4),
                rhs_scale=x_scales[(chunk, d)][:],
                start=True,
                stop=True,
            )

        def clip_log_sigma(step):
            chunk, d, kt = place(step)
            clipped[step] = work.tile([P, N_COLS], F32, name="clipped")
            nc.vector.tensor_scalar(
                out=clipped[step][:],
                in0=acc[(SIGMA, step, "")][:],
                scalar1=clip_low[:, d, kt : kt + 1],
                scalar2=clip_high[:, d, kt : kt + 1],
                op0=ALU.max,
                op1=ALU.min,
            )

        def exp_minus_log_sigma(step):
            chunk, d, kt = place(step)
            inv_sigma[step] = work.tile([P, N_COLS], F32, name="inv_sigma")
            nc.scalar.activation(
                out=inv_sigma[step][:],
                in_=clipped[step][:],
                func=ACT.Exp,
                bias=neg_b_sig[:, d, kt : kt + 1],
                scale=-1.0,
            )

        def mu_minus_y(step):
            chunk, d, kt = place(step)
            distance[step] = work.tile([P, N_COLS], F32, name="distance")
            nc.vector.scalar_tensor_tensor(
                out=distance[step][:],
                in0=acc[(MU, step, "")][:],
                scalar=bias[:, d, KT * MU + kt : KT * MU + kt + 1],
                in1=y_all[chunk][:, d, :],
                op0=ALU.add,
                op1=ALU.subtract,
            )

        def divide_by_sigma(step):
            z[step] = work.tile([P, N_COLS], F32, name="z")
            nc.gpsimd.tensor_tensor(
                out=z[step][:], in0=distance[step][:], in1=inv_sigma[step][:], op=ALU.mult
            )

        def square(step):
            half_z2[step] = work.tile([P, N_COLS], F32, name="half_z2")
            nc.scalar.activation(
                out=half_z2[step][:], in_=z[step][:], func=ACT.Square, scale=math.sqrt(0.5)
            )

        def add_penalty(step):
            penalty[step] = work.tile([P, N_COLS], F32, name="penalty")
            nc.gpsimd.tensor_tensor(
                out=penalty[step][:], in0=clipped[step][:], in1=half_z2[step][:], op=ALU.add
            )

        def make_a(step):
            chunk, d, kt = place(step)
            kept[(1, step)] = keep.tile([P, N_COLS], F32, name="a_tile")
            nc.scalar.activation(
                out=kept[(1, step)][:],
                in_=acc[(ALPHA, step, "a")][:],
                func=ACT.Identity,
                bias=bias[:, d, KT * ALPHA + kt : KT * ALPHA + kt + 1],
                scale=1.0,
            )

        def make_t(step):
            chunk, d, kt = place(step)
            kept[(0, step)] = keep.tile([P, N_COLS], F32, name="t_tile")
            nc.vector.scalar_tensor_tensor(
                out=kept[(0, step)][:],
                in0=acc[(ALPHA, step, "t")][:],
                scalar=b_alp_sig[:, d, kt : kt + 1],
                in1=penalty[step][:],
                op0=ALU.add,
                op1=ALU.subtract,
            )

        def statistic(tile_, kind, block):
            chunk, d, j = block // (D * BLOCKS), (block // BLOCKS) % D, block % BLOCKS
            column = chunk * BLOCKS + j
            return tile_[:, kind, d, column : column + 1]

        def turn(kind, block):
            first_step = (block // BLOCKS) * KT
            j = block % BLOCKS
            turned[(kind, block)] = tp_psum.tile([P, K], F32, name="turned", tag="bank")
            for kt in range(KT):
                nc.tensor.transpose(
                    out=turned[(kind, block)][:, kt * P : (kt + 1) * P],
                    in_=kept[(kind, first_step + kt)][:, j * P : (j + 1) * P],
                    identity=ident_f32[:],
                )

        def maximum(kind, block):
            nc.vector.tensor_reduce(
                out=statistic(neg_max, kind, block),
                in_=turned[(kind, block)][:],
                axis=AXIS.X,
                op=ALU.max,
                negate=True,
            )

        def sum_of_exp(kind, block):
            unread = work.tile([P, K], F32)
            nc.scalar.activation(
                out=unread[:],
                in_=turned[(kind, block)][:],
                func=ACT.Exp,
                bias=statistic(neg_max, kind, block),
                scale=1.0,
                accum_out=statistic(exp_sum, kind, block),
            )

        n_x_banks = N_CHUNKS * X_BANKS

        def is_step(step):
            return 0 <= step < STEPS

        def is_block(block):
            return 0 <= block < STEPS

        transpose_x_bank(0)
        transpose_x_bank(1)
        transpose_weight(SIGMA, 0)
        transpose_biases()
        empty_x_bank(0)
        empty_x_bank(1)
        quantise_weight(SIGMA, 0)
        quantise_x(0)
        bias_columns()
        transpose_weight(MU, 0)
        spread_y(0)
        quantise_weight(MU, 0)
        keep_y(0)
        product(SIGMA, 0)
        product(MU, 0)
        transpose_weight(ALPHA, 0)
        quantise_weight(ALPHA, 0)
        for w in (SIGMA, MU, ALPHA):
            transpose_weight(w, 1)
        transpose_x_bank(2)

        for i in range(STEPS + LAG_T + 2):
            if is_block(i - LAG_T):
                turn(0, i - LAG_T)
            if is_block(i - LAG_A):
                turn(1, i - LAG_A)
            if is_step(i - 2):
                square(i - 2)
            if is_step(i - 1):
                make_a(i - 1)
            if is_step(i):
                clip_log_sigma(i)
                mu_minus_y(i)

            if i + 1 < KT:
                for w in (SIGMA, MU, ALPHA):
                    quantise_weight(w, i + 1)
            if i % 2 == 0 and (i + 4) // 2 < n_x_banks:
                empty_x_bank((i + 4) // 2)
            if 1 <= i - 2 < N_CHUNKS:
                keep_y(i - 2)

            if is_step(i - 3):
                make_t(i - 3)
            if is_step(i + 1):
                product(SIGMA, i + 1)
                product(MU, i + 1)
            if is_step(i):
                product(ALPHA, i, "a")
            if is_step(i - 2):
                product(ALPHA, i - 2, "t")
            if is_step(i - 1):
                divide_by_sigma(i - 1)
            if is_step(i - 2):
                add_penalty(i - 2)

            if is_block(i - LAG_T):
                maximum(0, i - LAG_T)
            if is_block(i - LAG_A):
                maximum(1, i - LAG_A)
            if i % 4 == 2 and 1 <= (i + 2) // 4 < N_CHUNKS * D:
                quantise_x((i + 2) // 4)
            if is_block(i - LAG_T - 1):
                sum_of_exp(0, i - LAG_T - 1)
            if is_block(i - LAG_A - 1):
                sum_of_exp(1, i - LAG_A - 1)
            if is_step(i):
                exp_minus_log_sigma(i)

            if i + 2 < KT:
                for w in (SIGMA, MU, ALPHA):
                    transpose_weight(w, i + 2)
            if i % 2 == 1 and (i + 5) // 2 < n_x_banks:
                transpose_x_bank((i + 5) // 2)
            if 1 <= i - 1 < N_CHUNKS:
                spread_y(i - 1)

        log_sum = const.tile([P, 2, D, n_blocks], F32)
        nc.scalar.activation(out=log_sum[:], in_=exp_sum[:], func=ACT.Ln)
        lse = const.tile([P, 2, D, n_blocks], F32)
        nc.vector.tensor_tensor(out=lse[:], in0=log_sum[:], in1=neg_max[:], op=ALU.subtract)
        per_d = const.tile([P, D, n_blocks], F32)
        nc.vector.tensor_tensor(out=per_d[:], in0=lse[:, 0], in1=lse[:, 1], op=ALU.subtract)
        nc.vector.scalar_tensor_tensor(
            out=result[:, 0:n_blocks],
            in0=per_d[:, 0, :],
            scalar=-math.log(2.0 * math.pi),
            in1=per_d[:, 1, :],
            op0=ALU.add,
            op1=ALU.add,
        )
        result_bank = tp_psum.tile([P, P], F32, tag="bank")
        nc.tensor.transpose(out=result_bank[:], in_=result[:], identity=ident_f32[:])
        out_rows = const.tile([n_blocks, P], F32)
        nc.scalar.copy(out=out_rows[:], in_=result_bank[0:n_blocks, :])
        nc.sync.dma_start(out=out.rearrange("(j p) -> j p", p=P), in_=out_rows[:])
